import numpy as np
import ml_dtypes


def mxq(x, axis, fmt="e4m3"):
    dtype, down = {"e4m3": (ml_dtypes.float8_e4m3fn, 7), "e5m2": (ml_dtypes.float8_e5m2, 14)}[fmt]
    v = np.moveaxis(np.asarray(x, np.float32).astype(ml_dtypes.bfloat16).astype(np.float64), axis, -1)
    blocks = v.reshape(v.shape[:-1] + (-1, 32))
    amax = np.abs(blocks).max(-1, keepdims=True)
    byte = np.maximum(np.where(amax > 0, np.frexp(amax)[1] - 1 + 127, 0) - down, 1)
    scale = np.exp2(byte - 127.0)
    codes = (blocks / scale).astype(np.float32).astype(dtype).astype(np.float64)
    return np.moveaxis((codes * scale).reshape(v.shape), -1, axis)


WIDE = False


def mx_kscale(k):
    if not WIDE:
        return np.ones(k)
    levels = np.array([10, -10, 5, -5, 0])
    a = np.random.permutation(np.resize(levels, k // 512 * 4)).reshape(k // 512, 4)
    idx = np.arange(k)
    return np.exp2(a[idx // 512, idx % 128 // 32])


BF16 = ml_dtypes.bfloat16


def bf(x):
    return np.asarray(x, np.float32).astype(BF16)


def f64(x):
    return np.asarray(x).astype(np.float64)


B, K, N = 512, 16384, 512
NACT = 4


def setup_inputs():
    s = mx_kscale(K)
    g = np.tile(np.array([1.0, 1.0, 1.0, 0.5]), N // NACT)
    x = np.random.standard_normal((B, K)) * s
    weight = np.random.uniform(-1.0, 1.0, (N, K)) / np.sqrt(K) * g[:, None] / s[None, :]
    return {"x": bf(x), "weight": bf(weight)}


def reference(x, weight):
    y = mxq(f64(x), 1, "e4m3") @ mxq(f64(weight), 1, "e4m3").T
    rows, cols = y.shape
    y3 = y.reshape(rows, cols // NACT, NACT)
    out = np.stack(
        [y3[..., 0],
         np.cos(y3[..., 1]),
         np.sin(y3[..., 2]),
         np.tan(y3[..., 3])],
        axis=-1,
    )
    return out.reshape(rows, cols)

@@ -1,0 +1,150 @@
+import math
+from contextlib import ExitStack
+
+import concourse.mybir as mybir
+from concourse.masks import make_identity
+
+F32 = mybir.dt.float32
+BF16 = mybir.dt.bfloat16
+U32 = mybir.dt.uint32
+U8 = mybir.dt.uint8
+FP8X4 = mybir.dt.float8_e4m3fn_x4
+ALU = mybir.AluOpType
+ACT = mybir.ActivationFunctionType
+
+P = 128
+ROWS = 512
+K = 16384
+ROW_TILES = ROWS // P
+K_PASS = 4 * P
+PASSES = K // K_PASS
+WORDS_PASS = K_PASS // 2
+CHUNK_K = 1024
+PASSES_PER_CHUNK = CHUNK_K // K_PASS
+CHUNKS = K // CHUNK_K
+STAGE_BUFS = 6
+NACT = 4
+GROUPS = ROWS // NACT
+BANK = 512
+
+TWO_PI = 2.0 * math.pi
+ROUND_MAGIC = 1.5 * 2.0**23
+
+FLOPS = 2 * ROWS * ROWS * K
+
+
+def tile_mylayerfunc_k_kernel(tc, x, weight, out):
+    nc = tc.nc
+    with ExitStack() as ctx:
+        const = ctx.enter_context(tc.tile_pool(name="const", bufs=1))
+        stage = ctx.enter_context(tc.tile_pool(name="stage", bufs=STAGE_BUFS))
+        work = ctx.enter_context(tc.tile_pool(name="work", bufs=3))
+        tail = ctx.enter_context(tc.tile_pool(name="tail", bufs=2))
+        flip = ctx.enter_context(tc.psum_pool(name="flip", bufs=4))
+        sums = ctx.enter_context(tc.psum_pool(name="sums", bufs=1))
+        ctx.enter_context(tc.manual_schedule())
+
+        dram = {
+            "x": x.rearrange("(t p) k -> p t k", p=P),
+            "w": weight.rearrange("(t p) k -> p t k", p=P),
+        }
+        staged = {}
+
+        def load(c):
+            for name in ("x", "w"):
+                rows = stage.tile([P, ROW_TILES, CHUNK_K], BF16, name="rows_" + name)
+                nc.sync.dma_start(out=rows[:], in_=dram[name][:, :, c * CHUNK_K : (c + 1) * CHUNK_K])
+                staged[(name, c)] = rows
+
+        for c in range(STAGE_BUFS):
+            load(c)
+
+        ident = const.tile([P, P], F32, name="ident")
+        make_identity(nc, ident[:])
+
+        zero = const.tile([P, 1], F32, name="zero")
+        nc.vector.memset(zero[:], 0.0)
+        warm = const.tile([P, 1], F32, name="warm")
+        nc.scalar.activation(out=warm[:], in_=zero[:], func=ACT.Sin)
+
+        acc = [sums.tile([P, BANK], F32, name="acc%d" % t) for t in range(ROW_TILES)]
+        codes = {}
+
+        def multiply(g):
+            xc, xs, wc, ws = codes[g]
+            for t in range(ROW_TILES):
+                cols = slice(t * P, (t + 1) * P)
+                nc.tensor.matmul_mx(
+                    out=acc[t][:],
+                    lhsT=xc[:, cols].bitcast(FP8X4),
+                    lhsT_scale=xs[:, cols],
+                    rhs=wc[:].bitcast(FP8X4),
+                    rhs_scale=ws[:],
+                    start=(g == 0),
+                    stop=(g == PASSES - 1),
+                )
+
+        for g in range(PASSES):
+            c, gi = divmod(g, PASSES_PER_CHUNK)
+            banks = []
+            for name in ("x", "w"):
+                words = staged[(name, c)]
+                for half in range(2):
+                    bank = flip.tile([P, 2, 2, P], F32, name="bank")
+                    for r in range(2):
+                        row_words = words[:, 2 * half + r, :].bitcast(F32)
+                        for u in range(2):
+                            first = gi * WORDS_PASS + u * P
+                            nc.tensor.transpose(bank[:, r, u, :], row_words[:, first : first + P], ident[:])
+                    banks.append(bank)
+
+            if g > 0:
+                multiply(g - 1)
+
+            grouped = {}
+            for i, name in enumerate(("x", "w")):
+                grouped[name] = work.tile([P, ROWS * 4], BF16, name="grouped_" + name, align_bytes=64)
+                for half in range(2):
+                    b = 2 * i + half
+                    dst = grouped[name][:, half * 1024 : (half + 1) * 1024].bitcast(F32)
+                    dst = dst.rearrange("p (r m u) -> p r m u", r=2, u=2)
+                    src = banks[b][:].rearrange("p r u m -> p r m u")
+                    if b == 3:
+                        nc.vector.tensor_copy(out=dst, in_=src)
+                    else:
+                        nc.scalar.copy(out=dst, in_=src)
+
+            made = []
+            for name in ("x", "w"):
+                words4 = work.tile([P, ROWS], U32, name="codes_" + name, align_bytes=64)
+                scales = work.tile([P, ROWS], U8, name="scales_" + name, align_bytes=64)
+                nc.vector.quantize_mx(out=words4[:].bitcast(FP8X4), scales=scales[:], in_=grouped[name][:])
+                made.append(words4)
+                made.append(scales)
+            codes[g] = made
+
+            if gi == PASSES_PER_CHUNK - 1 and c + STAGE_BUFS < CHUNKS:
+                load(c + STAGE_BUFS)
+
+        multiply(PASSES - 1)
+
+        for t in range(ROW_TILES):
+            y = acc[t][:].rearrange("p (g c) -> p c g", c=NACT)
+            turns = tail.tile([P, 5, GROUPS], F32, name="turns")
+            res = tail.tile([P, 5, GROUPS], F32, name="res")
+            nc.scalar.activation(out=turns[:, 1:5:3, :], in_=y[:, 1:4:2, :], func=ACT.Copy, bias=0.25, scale=1.0 / TWO_PI)
+            nc.scalar.activation(out=turns[:, 2:4, :], in_=y[:, 2:4, :], func=ACT.Copy, scale=1.0 / TWO_PI)
+            nc.scalar.copy(out=res[:, 0, :], in_=y[:, 0, :])
+            whole = tail.tile([P, 4, GROUPS], F32, name="whole")
+            nc.vector.tensor_scalar(
+                out=whole[:], in0=turns[:, 1:5, :], scalar1=ROUND_MAGIC, scalar2=ROUND_MAGIC, op0=ALU.add, op1=ALU.subtract
+            )
+            frac = tail.tile([P, 4, GROUPS], F32, name="frac")
+            nc.vector.tensor_tensor(out=frac[:], in0=turns[:, 1:5, :], in1=whole[:], op=ALU.subtract)
+            nc.scalar.activation(out=res[:, 1:5, :], in_=frac[:], func=ACT.Sin, scale=TWO_PI)
+            sec = tail.tile([P, GROUPS], F32, name="sec")
+            nc.vector.reciprocal(out=sec[:], in_=res[:, 4, :])
+            nc.vector.tensor_mul(res[:, 3, :], res[:, 3, :], sec[:])
+            woven = tail.tile([P, GROUPS, NACT], F32, name="woven")
+            nc.vector.tensor_copy(out=woven[:], in_=res[:, 0:4, :].rearrange("p c g -> p g c"))
+            nc.sync.dma_start(out=out[t * P : (t + 1) * P, :], in_=woven[:].rearrange("p g c -> p (g c)"))

@@ -18,11 +18,13 @@ K = 16384
 ROW_TILES = ROWS // P
 K_PASS = 4 * P
 PASSES = K // K_PASS
-WORDS_PASS = K_PASS // 2
 CHUNK_K = 1024
 PASSES_PER_CHUNK = CHUNK_K // K_PASS
 CHUNKS = K // CHUNK_K
 STAGE_BUFS = 6
+UNIT = 4
+TAIL_PASSES = 2 * UNIT
+MAIN_PASSES = PASSES - TAIL_PASSES
 NACT = 4
 GROUPS = ROWS // NACT
 BANK = 512
@@ -39,8 +41,10 @@ def tile_mylayerfunc_k_kernel(tc, x, weight, out):
         const = ctx.enter_context(tc.tile_pool(name="const", bufs=1))
         stage = ctx.enter_context(tc.tile_pool(name="stage", bufs=STAGE_BUFS))
         work = ctx.enter_context(tc.tile_pool(name="work", bufs=3))
-        tail = ctx.enter_context(tc.tile_pool(name="tail", bufs=2))
-        flip = ctx.enter_context(tc.psum_pool(name="flip", bufs=4))
+        x_mx = ctx.enter_context(tc.tile_pool(name="x_mx", bufs=4))
+        w_mx = ctx.enter_context(tc.tile_pool(name="w_mx", bufs=TAIL_PASSES))
+        tail = ctx.enter_context(tc.tile_pool(name="tail", bufs=3))
+        flipped = ctx.enter_context(tc.psum_pool(name="flipped", bufs=4))
         sums = ctx.enter_context(tc.psum_pool(name="sums", bufs=1))
         ctx.enter_context(tc.manual_schedule())
 
@@ -48,6 +52,7 @@ def tile_mylayerfunc_k_kernel(tc, x, weight, out):
             "x": x.rearrange("(t p) k -> p t k", p=P),
             "w": weight.rearrange("(t p) k -> p t k", p=P),
         }
+        mx_pool = {"x": x_mx, "w": w_mx}
         staged = {}
 
         def load(c):
@@ -55,6 +60,10 @@ def tile_mylayerfunc_k_kernel(tc, x, weight, out):
                 rows = stage.tile([P, ROW_TILES, CHUNK_K], BF16, name="rows_" + name)
                 nc.sync.dma_start(out=rows[:], in_=dram[name][:, :, c * CHUNK_K : (c + 1) * CHUNK_K])
                 staged[(name, c)] = rows
+
+        def block(name, t, g):
+            c, gi = divmod(g, PASSES_PER_CHUNK)
+            return staged[(name, c)][:, t, gi * K_PASS : (gi + 1) * K_PASS].bitcast(F32)
 
         for c in range(STAGE_BUFS):
             load(c)
@@ -68,67 +77,81 @@ def tile_mylayerfunc_k_kernel(tc, x, weight, out):
         nc.scalar.activation(out=warm[:], in_=zero[:], func=ACT.Sin)
 
         acc = [sums.tile([P, BANK], F32, name="acc%d" % t) for t in range(ROW_TILES)]
-        codes = {}
 
-        def multiply(g):
-            xc, xs, wc, ws = codes[g]
-            for t in range(ROW_TILES):
-                cols = slice(t * P, (t + 1) * P)
-                nc.tensor.matmul_mx(
-                    out=acc[t][:],
-                    lhsT=xc[:, cols].bitcast(FP8X4),
-                    lhsT_scale=xs[:, cols],
-                    rhs=wc[:].bitcast(FP8X4),
-                    rhs_scale=ws[:],
-                    start=(g == 0),
-                    stop=(g == PASSES - 1),
-                )
-
-        for g in range(PASSES):
-            c, gi = divmod(g, PASSES_PER_CHUNK)
+        def flip(blocks):
             banks = []
-            for name in ("x", "w"):
-                words = staged[(name, c)]
-                for half in range(2):
-                    bank = flip.tile([P, 2, 2, P], F32, name="bank")
-                    for r in range(2):
-                        row_words = words[:, 2 * half + r, :].bitcast(F32)
-                        for u in range(2):
-                            first = gi * WORDS_PASS + u * P
-                            nc.tensor.transpose(bank[:, r, u, :], row_words[:, first : first + P], ident[:])
-                    banks.append(bank)
+            for half in range(2):
+                bank = flipped.tile([P, 2, 2, P], F32, name="bank")
+                for r in range(2):
+                    for u in range(2):
+                        nc.tensor.transpose(bank[:, r, u, :], blocks[2 * half + r][:, u * P : (u + 1) * P], ident[:])
+                banks.append(bank)
+            return banks
 
+        def regroup(banks, name, engines):
+            grouped = work.tile([P, UNIT * P * 4], BF16, name="grouped_" + name, align_bytes=64)
+            for half in range(2):
+                dst = grouped[:, half * 1024 : (half + 1) * 1024].bitcast(F32)
+                dst = dst.rearrange("p (r m u) -> p r m u", r=2, u=2)
+                src = banks[half][:].rearrange("p r u m -> p r m u")
+                if engines[half] == "vector":
+                    nc.vector.tensor_copy(out=dst, in_=src)
+                else:
+                    nc.scalar.copy(out=dst, in_=src)
+            return grouped
+
+        def quantise(grouped, name):
+            codes = mx_pool[name].tile([P, UNIT * P], U32, name="codes_" + name, align_bytes=64)
+            scales = mx_pool[name].tile([P, UNIT * P], U8, name="scales_" + name, align_bytes=64)
+            nc.vector.quantize_mx(out=codes[:].bitcast(FP8X4), scales=scales[:], in_=grouped[:])
+            return codes, scales
+
+        def pack_round(banks, names):
+            first = regroup(banks[0:2], names[0], ("scalar", "scalar"))
+            second = regroup(banks[2:4], names[1], ("scalar", "vector"))
+            return quantise(first, names[0]), quantise(second, names[1])
+
+        def mx_pass(t, x_unit, j, w_unit, start, stop):
+            cols = slice(j * P, (j + 1) * P)
+            nc.tensor.matmul_mx(
+                out=acc[t][:],
+                lhsT=x_unit[0][:, cols].bitcast(FP8X4),
+                lhsT_scale=x_unit[1][:, cols],
+                rhs=w_unit[0][:].bitcast(FP8X4),
+                rhs_scale=w_unit[1][:],
+                start=start,
+                stop=stop,
+            )
+
+        x_units = {}
+        w_units = {}
+
+        def multiply_pass(g):
+            for t in range(ROW_TILES):
+                mx_pass(t, x_units[g], t, w_units[g], g == 0, False)
+
+        for g in range(MAIN_PASSES):
+            banks = flip([block("x", t, g) for t in range(ROW_TILES)])
+            banks += flip([block("w", t, g) for t in range(ROW_TILES)])
             if g > 0:
-                multiply(g - 1)
-
-            grouped = {}
-            for i, name in enumerate(("x", "w")):
-                grouped[name] = work.tile([P, ROWS * 4], BF16, name="grouped_" + name, align_bytes=64)
-                for half in range(2):
-                    b = 2 * i + half
-                    dst = grouped[name][:, half * 1024 : (half + 1) * 1024].bitcast(F32)
-                    dst = dst.rearrange("p (r m u) -> p r m u", r=2, u=2)
-                    src = banks[b][:].rearrange("p r u m -> p r m u")
-                    if b == 3:
-                        nc.vector.tensor_copy(out=dst, in_=src)
-                    else:
-                        nc.scalar.copy(out=dst, in_=src)
-
-            made = []
-            for name in ("x", "w"):
-                words4 = work.tile([P, ROWS], U32, name="codes_" + name, align_bytes=64)
-                scales = work.tile([P, ROWS], U8, name="scales_" + name, align_bytes=64)
-                nc.vector.quantize_mx(out=words4[:].bitcast(FP8X4), scales=scales[:], in_=grouped[name][:])
-                made.append(words4)
-                made.append(scales)
-            codes[g] = made
-
+                multiply_pass(g - 1)
+            x_units[g], w_units[g] = pack_round(banks, ("x", "w"))
+            c, gi = divmod(g, PASSES_PER_CHUNK)
             if gi == PASSES_PER_CHUNK - 1 and c + STAGE_BUFS < CHUNKS:
                 load(c + STAGE_BUFS)
 
-        multiply(PASSES - 1)
+        for g in range(MAIN_PASSES, PASSES, 2):
+            banks = flip([block("w", t, g) for t in range(ROW_TILES)])
+            banks += flip([block("w", t, g + 1) for t in range(ROW_TILES)])
+            if g == MAIN_PASSES:
+                multiply_pass(g - 1)
+            w_units[g], w_units[g + 1] = pack_round(banks, ("w", "w"))
 
-        for t in range(ROW_TILES):
+        def multiply_tile(t, units):
+            for j in range(TAIL_PASSES):
+                mx_pass(t, units[j // UNIT], j % UNIT, w_units[MAIN_PASSES + j], False, j == TAIL_PASSES - 1)
+
+        def angles(t):
             y = acc[t][:].rearrange("p (g c) -> p c g", c=NACT)
             turns = tail.tile([P, 5, GROUPS], F32, name="turns")
             res = tail.tile([P, 5, GROUPS], F32, name="res")
@@ -141,6 +164,9 @@ def tile_mylayerfunc_k_kernel(tc, x, weight, out):
             )
             frac = tail.tile([P, 4, GROUPS], F32, name="frac")
             nc.vector.tensor_tensor(out=frac[:], in0=turns[:, 1:5, :], in1=whole[:], op=ALU.subtract)
+            return frac, res
+
+        def finish(t, frac, res):
             nc.scalar.activation(out=res[:, 1:5, :], in_=frac[:], func=ACT.Sin, scale=TWO_PI)
             sec = tail.tile([P, GROUPS], F32, name="sec")
             nc.vector.reciprocal(out=sec[:], in_=res[:, 4, :])
@@ -148,3 +174,18 @@ def tile_mylayerfunc_k_kernel(tc, x, weight, out):
             woven = tail.tile([P, GROUPS, NACT], F32, name="woven")
             nc.vector.tensor_copy(out=woven[:], in_=res[:, 0:4, :].rearrange("p c g -> p g c"))
             nc.sync.dma_start(out=out[t * P : (t + 1) * P, :], in_=woven[:].rearrange("p g c -> p (g c)"))
+
+        tile_units = {}
+        halfway = {}
+        for i in range(ROW_TILES + 2):
+            if i < ROW_TILES:
+                banks = flip([block("x", i, MAIN_PASSES + j) for j in range(UNIT)])
+                banks += flip([block("x", i, MAIN_PASSES + UNIT + j) for j in range(UNIT)])
+            if 1 <= i <= ROW_TILES:
+                multiply_tile(i - 1, tile_units[i - 1])
+            if i < ROW_TILES:
+                tile_units[i] = pack_round(banks, ("x", "x"))
+            if i >= 2:
+                finish(i - 2, halfway[i - 2][0], halfway[i - 2][1])
+            if 1 <= i <= ROW_TILES:
+                halfway[i - 1] = angles(i - 1)

@@ -42,7 +42,8 @@ def tile_mylayerfunc_k_kernel(tc, x, weight, out):
         stage = ctx.enter_context(tc.tile_pool(name="stage", bufs=STAGE_BUFS))
         work = ctx.enter_context(tc.tile_pool(name="work", bufs=3))
         x_mx = ctx.enter_context(tc.tile_pool(name="x_mx", bufs=4))
-        w_mx = ctx.enter_context(tc.tile_pool(name="w_mx", bufs=TAIL_PASSES))
+        w_mx = ctx.enter_context(tc.tile_pool(name="w_mx", bufs=3))
+        w_last = ctx.enter_context(tc.tile_pool(name="w_last", bufs=TAIL_PASSES))
         tail = ctx.enter_context(tc.tile_pool(name="tail", bufs=3))
         flipped = ctx.enter_context(tc.psum_pool(name="flipped", bufs=4))
         sums = ctx.enter_context(tc.psum_pool(name="sums", bufs=1))
@@ -52,7 +53,7 @@ def tile_mylayerfunc_k_kernel(tc, x, weight, out):
             "x": x.rearrange("(t p) k -> p t k", p=P),
             "w": weight.rearrange("(t p) k -> p t k", p=P),
         }
-        mx_pool = {"x": x_mx, "w": w_mx}
+        mx_pool = {"x": x_mx, "w": w_mx, "w_last": w_last}
         staged = {}
 
         def load(c):
@@ -106,10 +107,10 @@ def tile_mylayerfunc_k_kernel(tc, x, weight, out):
             nc.vector.quantize_mx(out=codes[:].bitcast(FP8X4), scales=scales[:], in_=grouped[:])
             return codes, scales
 
-        def pack_round(banks, names):
-            first = regroup(banks[0:2], names[0], ("scalar", "scalar"))
-            second = regroup(banks[2:4], names[1], ("scalar", "vector"))
-            return quantise(first, names[0]), quantise(second, names[1])
+        def empty_round(banks, last_engine):
+            first = regroup(banks[0:2], "a", ("scalar", "scalar"))
+            second = regroup(banks[2:4], "b", ("scalar", last_engine))
+            return first, second
 
         def mx_pass(t, x_unit, j, w_unit, start, stop):
             cols = slice(j * P, (j + 1) * P)
@@ -133,19 +134,22 @@ def tile_mylayerfunc_k_kernel(tc, x, weight, out):
         for g in range(MAIN_PASSES):
             banks = flip([block("x", t, g) for t in range(ROW_TILES)])
             banks += flip([block("w", t, g) for t in range(ROW_TILES)])
+            x_grouped, w_grouped = empty_round(banks, "vector")
+            ahead = MAIN_PASSES + 2 * (g - (MAIN_PASSES - TAIL_PASSES // 2))
+            if ahead >= MAIN_PASSES:
+                banks = flip([block("w", t, ahead) for t in range(ROW_TILES)])
+                banks += flip([block("w", t, ahead + 1) for t in range(ROW_TILES)])
             if g > 0:
                 multiply_pass(g - 1)
-            x_units[g], w_units[g] = pack_round(banks, ("x", "w"))
+            x_units[g] = quantise(x_grouped, "x")
+            w_units[g] = quantise(w_grouped, "w")
+            if ahead >= MAIN_PASSES:
+                first, second = empty_round(banks, "vector")
+                w_units[ahead] = quantise(first, "w_last")
+                w_units[ahead + 1] = quantise(second, "w_last")
             c, gi = divmod(g, PASSES_PER_CHUNK)
             if gi == PASSES_PER_CHUNK - 1 and c + STAGE_BUFS < CHUNKS:
                 load(c + STAGE_BUFS)
-
-        for g in range(MAIN_PASSES, PASSES, 2):
-            banks = flip([block("w", t, g) for t in range(ROW_TILES)])
-            banks += flip([block("w", t, g + 1) for t in range(ROW_TILES)])
-            if g == MAIN_PASSES:
-                multiply_pass(g - 1)
-            w_units[g], w_units[g + 1] = pack_round(banks, ("w", "w"))
 
         def multiply_tile(t, units):
             for j in range(TAIL_PASSES):
@@ -167,7 +171,8 @@ def tile_mylayerfunc_k_kernel(tc, x, weight, out):
             return frac, res
 
         def finish(t, frac, res):
-            nc.scalar.activation(out=res[:, 1:5, :], in_=frac[:], func=ACT.Sin, scale=TWO_PI)
+            nc.scalar.activation(out=res[:, 4, :], in_=frac[:, 3, :], func=ACT.Sin, scale=TWO_PI)
+            nc.scalar.activation(out=res[:, 1:4, :], in_=frac[:, 0:3, :], func=ACT.Sin, scale=TWO_PI)
             sec = tail.tile([P, GROUPS], F32, name="sec")
             nc.vector.reciprocal(out=sec[:], in_=res[:, 4, :])
             nc.vector.tensor_mul(res[:, 3, :], res[:, 3, :], sec[:])
@@ -181,10 +186,13 @@ def tile_mylayerfunc_k_kernel(tc, x, weight, out):
             if i < ROW_TILES:
                 banks = flip([block("x", i, MAIN_PASSES + j) for j in range(UNIT)])
                 banks += flip([block("x", i, MAIN_PASSES + UNIT + j) for j in range(UNIT)])
+            if i == 0:
+                multiply_pass(MAIN_PASSES - 1)
             if 1 <= i <= ROW_TILES:
                 multiply_tile(i - 1, tile_units[i - 1])
             if i < ROW_TILES:
-                tile_units[i] = pack_round(banks, ("x", "x"))
+                first, second = empty_round(banks, "scalar")
+                tile_units[i] = (quantise(first, "x"), quantise(second, "x"))
             if i >= 2:
                 finish(i - 2, halfway[i - 2][0], halfway[i - 2][1])
             if 1 <= i <= ROW_TILES:

@@ -25,6 +25,7 @@ STAGE_BUFS = 6
 UNIT = 4
 TAIL_PASSES = 2 * UNIT
 MAIN_PASSES = PASSES - TAIL_PASSES
+LAG = 2
 NACT = 4
 GROUPS = ROWS // NACT
 BANK = 512
@@ -42,7 +43,7 @@ def tile_mylayerfunc_k_kernel(tc, x, weight, out):
         stage = ctx.enter_context(tc.tile_pool(name="stage", bufs=STAGE_BUFS))
         work = ctx.enter_context(tc.tile_pool(name="work", bufs=3))
         x_mx = ctx.enter_context(tc.tile_pool(name="x_mx", bufs=4))
-        w_mx = ctx.enter_context(tc.tile_pool(name="w_mx", bufs=3))
+        w_mx = ctx.enter_context(tc.tile_pool(name="w_mx", bufs=4))
         w_last = ctx.enter_context(tc.tile_pool(name="w_last", bufs=TAIL_PASSES))
         tail = ctx.enter_context(tc.tile_pool(name="tail", bufs=3))
         flipped = ctx.enter_context(tc.psum_pool(name="flipped", bufs=4))
@@ -139,8 +140,8 @@ def tile_mylayerfunc_k_kernel(tc, x, weight, out):
             if ahead >= MAIN_PASSES:
                 banks = flip([block("w", t, ahead) for t in range(ROW_TILES)])
                 banks += flip([block("w", t, ahead + 1) for t in range(ROW_TILES)])
-            if g > 0:
-                multiply_pass(g - 1)
+            if g >= LAG:
+                multiply_pass(g - LAG)
             x_units[g] = quantise(x_grouped, "x")
             w_units[g] = quantise(w_grouped, "w")
             if ahead >= MAIN_PASSES:
@@ -187,7 +188,8 @@ def tile_mylayerfunc_k_kernel(tc, x, weight, out):
                 banks = flip([block("x", i, MAIN_PASSES + j) for j in range(UNIT)])
                 banks += flip([block("x", i, MAIN_PASSES + UNIT + j) for j in range(UNIT)])
             if i == 0:
-                multiply_pass(MAIN_PASSES - 1)
+                for g in range(MAIN_PASSES - LAG, MAIN_PASSES):
+                    multiply_pass(g)
             if 1 <= i <= ROW_TILES:
                 multiply_tile(i - 1, tile_units[i - 1])
             if i < ROW_TILES:

import math
from contextlib import ExitStack

import concourse.mybir as mybir
from concourse.masks import make_identity

F32 = mybir.dt.float32
BF16 = mybir.dt.bfloat16
U32 = mybir.dt.uint32
U8 = mybir.dt.uint8
FP8X4 = mybir.dt.float8_e4m3fn_x4
ALU = mybir.AluOpType
ACT = mybir.ActivationFunctionType

P = 128
ROWS = 512
K = 16384
ROW_TILES = ROWS // P
K_PASS = 4 * P
PASSES = K // K_PASS
CHUNK_K = 1024
PASSES_PER_CHUNK = CHUNK_K // K_PASS
CHUNKS = K // CHUNK_K
STAGE_BUFS = 6
UNIT = 4
TAIL_PASSES = 2 * UNIT
MAIN_PASSES = PASSES - TAIL_PASSES
LAG = 2
NACT = 4
GROUPS = ROWS // NACT
BANK = 512

TWO_PI = 2.0 * math.pi
ROUND_MAGIC = 1.5 * 2.0**23

FLOPS = 2 * ROWS * ROWS * K


def tile_mylayerfunc_k_kernel(tc, x, weight, out):
    nc = tc.nc
    with ExitStack() as ctx:
        const = ctx.enter_context(tc.tile_pool(name="const", bufs=1))
        stage = ctx.enter_context(tc.tile_pool(name="stage", bufs=STAGE_BUFS))
        work = ctx.enter_context(tc.tile_pool(name="work", bufs=3))
        x_mx = ctx.enter_context(tc.tile_pool(name="x_mx", bufs=4))
        w_mx = ctx.enter_context(tc.tile_pool(name="w_mx", bufs=4))
        w_last = ctx.enter_context(tc.tile_pool(name="w_last", bufs=TAIL_PASSES))
        tail = ctx.enter_context(tc.tile_pool(name="tail", bufs=3))
        flipped = ctx.enter_context(tc.psum_pool(name="flipped", bufs=4))
        sums = ctx.enter_context(tc.psum_pool(name="sums", bufs=1))
        ctx.enter_context(tc.manual_schedule())

        dram = {
            "x": x.rearrange("(t p) k -> p t k", p=P),
            "w": weight.rearrange("(t p) k -> p t k", p=P),
        }
        mx_pool = {"x": x_mx, "w": w_mx, "w_last": w_last}
        staged = {}

        def load(c):
            for name in ("x", "w"):
                rows = stage.tile([P, ROW_TILES, CHUNK_K], BF16, name="rows_" + name)
                nc.sync.dma_start(out=rows[:], in_=dram[name][:, :, c * CHUNK_K : (c + 1) * CHUNK_K])
                staged[(name, c)] = rows

        def block(name, t, g):
            c, gi = divmod(g, PASSES_PER_CHUNK)
            return staged[(name, c)][:, t, gi * K_PASS : (gi + 1) * K_PASS].bitcast(F32)

        for c in range(STAGE_BUFS):
            load(c)

        ident = const.tile([P, P], F32, name="ident")
        make_identity(nc, ident[:])

        zero = const.tile([P, 1], F32, name="zero")
        nc.vector.memset(zero[:], 0.0)
        warm = const.tile([P, 1], F32, name="warm")
        nc.scalar.activation(out=warm[:], in_=zero[:], func=ACT.Sin)

        acc = [sums.tile([P, BANK], F32, name="acc%d" % t) for t in range(ROW_TILES)]

        def flip(blocks):
            banks = []
            for half in range(2):
                bank = flipped.tile([P, 2, 2, P], F32, name="bank")
                for r in range(2):
                    for u in range(2):
                        nc.tensor.transpose(bank[:, r, u, :], blocks[2 * half + r][:, u * P : (u + 1) * P], ident[:])
                banks.append(bank)
            return banks

        def regroup(banks, name, engines):
            grouped = work.tile([P, UNIT * P * 4], BF16, name="grouped_" + name, align_bytes=64)
            for half in range(2):
                dst = grouped[:, half * 1024 : (half + 1) * 1024].bitcast(F32)
                dst = dst.rearrange("p (r m u) -> p r m u", r=2, u=2)
                src = banks[half][:].rearrange("p r u m -> p r m u")
                if engines[half] == "vector":
                    nc.vector.tensor_copy(out=dst, in_=src)
                else:
                    nc.scalar.copy(out=dst, in_=src)
            return grouped

        def quantise(grouped, name):
            codes = mx_pool[name].tile([P, UNIT * P], U32, name="codes_" + name, align_bytes=64)
            scales = mx_pool[name].tile([P, UNIT * P], U8, name="scales_" + name, align_bytes=64)
            nc.vector.quantize_mx(out=codes[:].bitcast(FP8X4), scales=scales[:], in_=grouped[:])
            return codes, scales

        def empty_round(banks, last_engine):
            first = regroup(banks[0:2], "a", ("scalar", "scalar"))
            second = regroup(banks[2:4], "b", ("scalar", last_engine))
            return first, second

        def mx_pass(t, x_unit, j, w_unit, start, stop):
            cols = slice(j * P, (j + 1) * P)
            nc.tensor.matmul_mx(
                out=acc[t][:],
                lhsT=x_unit[0][:, cols].bitcast(FP8X4),
                lhsT_scale=x_unit[1][:, cols],
                rhs=w_unit[0][:].bitcast(FP8X4),
                rhs_scale=w_unit[1][:],
                start=start,
                stop=stop,
            )

        x_units = {}
        w_units = {}

        def multiply_pass(g):
            for t in range(ROW_TILES):
                mx_pass(t, x_units[g], t, w_units[g], g == 0, False)

        for g in range(MAIN_PASSES):
            banks = flip([block("x", t, g) for t in range(ROW_TILES)])
            banks += flip([block("w", t, g) for t in range(ROW_TILES)])
            x_grouped, w_grouped = empty_round(banks, "vector")
            ahead = MAIN_PASSES + 2 * (g - (MAIN_PASSES - TAIL_PASSES // 2))
            if ahead >= MAIN_PASSES:
                banks = flip([block("w", t, ahead) for t in range(ROW_TILES)])
                banks += flip([block("w", t, ahead + 1) for t in range(ROW_TILES)])
            if g >= LAG:
                multiply_pass(g - LAG)
            x_units[g] = quantise(x_grouped, "x")
            w_units[g] = quantise(w_grouped, "w")
            if ahead >= MAIN_PASSES:
                first, second = empty_round(banks, "vector")
                w_units[ahead] = quantise(first, "w_last")
                w_units[ahead + 1] = quantise(second, "w_last")
            c, gi = divmod(g, PASSES_PER_CHUNK)
            if gi == PASSES_PER_CHUNK - 1 and c + STAGE_BUFS < CHUNKS:
                load(c + STAGE_BUFS)

        def multiply_tile(t, units):
            for j in range(TAIL_PASSES):
                mx_pass(t, units[j // UNIT], j % UNIT, w_units[MAIN_PASSES + j], False, j == TAIL_PASSES - 1)

        def angles(t):
            y = acc[t][:].rearrange("p (g c) -> p c g", c=NACT)
            turns = tail.tile([P, 5, GROUPS], F32, name="turns")
            res = tail.tile([P, 5, GROUPS], F32, name="res")
            nc.scalar.activation(out=turns[:, 1:5:3, :], in_=y[:, 1:4:2, :], func=ACT.Copy, bias=0.25, scale=1.0 / TWO_PI)
            nc.scalar.activation(out=turns[:, 2:4, :], in_=y[:, 2:4, :], func=ACT.Copy, scale=1.0 / TWO_PI)
            nc.scalar.copy(out=res[:, 0, :], in_=y[:, 0, :])
            whole = tail.tile([P, 4, GROUPS], F32, name="whole")
            nc.vector.tensor_scalar(
                out=whole[:], in0=turns[:, 1:5, :], scalar1=ROUND_MAGIC, scalar2=ROUND_MAGIC, op0=ALU.add, op1=ALU.subtract
            )
            frac = tail.tile([P, 4, GROUPS], F32, name="frac")
            nc.vector.tensor_tensor(out=frac[:], in0=turns[:, 1:5, :], in1=whole[:], op=ALU.subtract)
            return frac, res

        def finish(t, frac, res):
            nc.scalar.activation(out=res[:, 4, :], in_=frac[:, 3, :], func=ACT.Sin, scale=TWO_PI)
            nc.scalar.activation(out=res[:, 1:4, :], in_=frac[:, 0:3, :], func=ACT.Sin, scale=TWO_PI)
            sec = tail.tile([P, GROUPS], F32, name="sec")
            nc.vector.reciprocal(out=sec[:], in_=res[:, 4, :])
            nc.vector.tensor_mul(res[:, 3, :], res[:, 3, :], sec[:])
            woven = tail.tile([P, GROUPS, NACT], F32, name="woven")
            nc.vector.tensor_copy(out=woven[:], in_=res[:, 0:4, :].rearrange("p c g -> p g c"))
            nc.sync.dma_start(out=out[t * P : (t + 1) * P, :], in_=woven[:].rearrange("p g c -> p (g c)"))

        tile_units = {}
        halfway = {}
        for i in range(ROW_TILES + 2):
            if i < ROW_TILES:
                banks = flip([block("x", i, MAIN_PASSES + j) for j in range(UNIT)])
                banks += flip([block("x", i, MAIN_PASSES + UNIT + j) for j in range(UNIT)])
            if i == 0:
                for g in range(MAIN_PASSES - LAG, MAIN_PASSES):
                    multiply_pass(g)
            if 1 <= i <= ROW_TILES:
                multiply_tile(i - 1, tile_units[i - 1])
            if i < ROW_TILES:
                first, second = empty_round(banks, "scalar")
                tile_units[i] = (quantise(first, "x"), quantise(second, "x"))
            if i >= 2:
                finish(i - 2, halfway[i - 2][0], halfway[i - 2][1])
            if 1 <= i <= ROW_TILES:
                halfway[i - 1] = angles(i - 1)
